import numpy as np
import ml_dtypes


def mxq(x, axis, fmt="e4m3"):
    dtype, down = {"e4m3": (ml_dtypes.float8_e4m3fn, 7), "e5m2": (ml_dtypes.float8_e5m2, 14)}[fmt]
    v = np.moveaxis(np.asarray(x, np.float32).astype(ml_dtypes.bfloat16).astype(np.float64), axis, -1)
    blocks = v.reshape(v.shape[:-1] + (-1, 32))
    amax = np.abs(blocks).max(-1, keepdims=True)
    byte = np.maximum(np.where(amax > 0, np.frexp(amax)[1] - 1 + 127, 0) - down, 1)
    scale = np.exp2(byte - 127.0)
    codes = (blocks / scale).astype(np.float32).astype(dtype).astype(np.float64)
    return np.moveaxis((codes * scale).reshape(v.shape), -1, axis)


WIDE = False


def mx_kscale(k):
    if not WIDE:
        return np.ones(k)
    levels = np.array([10, -10, 5, -5, 0])
    a = np.random.permutation(np.resize(levels, k // 512 * 4)).reshape(k // 512, 4)
    idx = np.arange(k)
    return np.exp2(a[idx // 512, idx % 128 // 32])


BF16 = ml_dtypes.bfloat16


def bf(x):
    return np.asarray(x, np.float32).astype(BF16)


def f64(x):
    return np.asarray(x).astype(np.float64)


E2M1 = np.array([0.0, 0.5, 1.0, 1.5, 2.0, 3.0, 4.0, 6.0, -0.0, -0.5, -1.0, -1.5, -2.0, -3.0, -4.0, -6.0])


def pack_weight(w, fmt):
    k, n = w.shape
    w = f64(bf(w)).reshape(k // 32, 32, n)
    amax = np.abs(w).max(1)
    if fmt == "e4m3":
        byte = np.frexp(amax)[1] - 1 + 127 - 7
    else:
        mant, ex = np.frexp(amax / 6.0)
        byte = np.where(mant > 0.5, ex, ex - 1) + 127
    byte = np.clip(np.where(amax > 0, byte, 1), 1, 254)
    scaled = (w * np.exp2(127.0 - byte)[:, None, :]).reshape(k, n).astype(np.float32)
    by_word = np.ascontiguousarray(scaled.reshape(k // 512, 128, 4, n).transpose(0, 1, 3, 2))
    if fmt == "e4m3":
        words = by_word.astype(ml_dtypes.float8_e4m3fn).view(np.uint8)
    else:
        c = by_word.astype(ml_dtypes.float4_e2m1fn).view(np.uint8) & 0xF
        words = c[..., 0::2] | (c[..., 1::2] << 4)
    return np.ascontiguousarray(words), np.ascontiguousarray(byte.astype(np.uint8).reshape(k // 512, 16, n))


def unpack_weight(words, scales, fmt):
    g, p, n, _ = words.shape
    if fmt == "e4m3":
        vals = np.ascontiguousarray(words).view(ml_dtypes.float8_e4m3fn).astype(np.float64)
    else:
        nib = np.empty((g, p, n, 4), np.uint8)
        nib[..., 0::2] = words & 0xF
        nib[..., 1::2] = words >> 4
        vals = E2M1[nib]
    vals = vals * np.repeat(np.exp2(scales.astype(np.float64) - 127.0), 8, axis=1)[..., None]
    return vals.transpose(0, 1, 3, 2).reshape(g * 512, n)


B, S, I, O = 2, 256, 2048, 5632


def setup_inputs():
    s = mx_kscale(I)
    x = bf(np.random.standard_normal((B, S, I)) * s)
    W = np.random.standard_normal((I, O)) * 0.022 / s[:, None]
    w_words, w_scales = pack_weight(W, "e4m3")
    return {"input": x, "bias": bf(np.random.standard_normal(O) * 0.3), "w_words": w_words, "w_scales": w_scales}


def reference(input, bias, w_words, w_scales):
    w = unpack_weight(w_words, w_scales, "e4m3")
    return (mxq(f64(input), 2, "e4m3") @ w) + f64(bias)

@@ -1,0 +1,243 @@
+from contextlib import ExitStack
+
+import concourse.mybir as mybir
+from concourse.masks import make_identity
+
+F32 = mybir.dt.float32
+BF16 = mybir.dt.bfloat16
+I32 = mybir.dt.int32
+U32 = mybir.dt.uint32
+U8 = mybir.dt.uint8
+FP8X4 = mybir.dt.float8_e4m3fn_x4
+ADD = mybir.AluOpType.add
+
+P = 128
+M = 512
+K = 2048
+N = 5632
+G = K // 512
+MT = M // P
+NT = 512
+NTILES = N // NT
+
+FLOPS = 2 * M * K * N
+
+CHUNKS = [[0], [1], [2], [3, 4], [5, 6], [7, 8, 9, 10]]
+SCALE_GROUPS = [(0, 3, 0), (3, 7, 3), (7, 11, 4)]
+SLAB_GROUPS = [[0, 1, 2, 3], [4, 5, 6, 7], [8, 9, 10]]
+BIAS_PIECES = [(0, 1024), (1024, 2048), (2048, 4096), (4096, 5632)]
+
+
+def tile_mxlinear_kernel(tc, x_in, bias, w_words, w_scales, out):
+    nc = tc.nc
+    x2d = x_in.flatten_outer_dims()
+    out2d = out.flatten_outer_dims()
+    w_i32 = w_words.rearrange("g p n t -> g p (n t)").bitcast(I32)
+    s_i32 = w_scales.bitcast(I32)
+
+    with ExitStack() as ctx:
+        keep = ctx.enter_context(tc.tile_pool(name="keep", bufs=1))
+        slabs = ctx.enter_context(tc.tile_pool(name="slabs", bufs=8))
+        psum = ctx.enter_context(tc.psum_pool(name="psum", bufs=8))
+        ctx.enter_context(tc.manual_schedule())
+
+        ident = keep.tile([P, P], F32, name="ident")
+        b_raw = keep.tile([P, 64], BF16, name="b_raw")
+        b_rep = keep.tile([P, 2, 4, 32], F32, name="b_rep")
+        bt_sb = keep.tile([P, N // 32], F32, name="bt_sb")
+        b_spread = keep.tile([P, N], BF16, name="b_spread", align_bytes=64)
+        bias_bc = keep.tile([P, N], BF16, name="bias_bc", align_bytes=64)
+        w_pl = keep.tile([P, N], U8, name="w_pl", align_bytes=64)
+        x_sb = []
+        grouped = []
+        x_codes = []
+        x_pl = []
+        for i in range(MT):
+            x_sb.append(keep.tile([P, K], BF16, name="x_sb%d" % i))
+            grouped.append(keep.tile([P, G, P, 4], BF16, name="grouped%d" % i, align_bytes=64))
+            x_codes.append(keep.tile([P, G * P], U32, name="x_codes%d" % i, align_bytes=64))
+            x_pl.append(keep.tile([P, G * P], U8, name="x_pl%d" % i, align_bytes=64))
+
+        nc.vector.memset(b_raw[:], 0.0)
+        nc.vector.memset(w_pl[:].bitcast(I32), 0)
+        make_identity(nc, ident[:])
+        nc.scalar.dma_start(out=b_raw[0:88, :], in_=bias.rearrange("(c e) -> c e", e=64))
+
+        for i in range(MT):
+            nc.sync.dma_start(out=x_sb[i][:], in_=x2d[i * P : (i + 1) * P, :])
+
+        w_slice = {}
+        for c, tiles in enumerate(CHUNKS):
+            for t0, t1, before in SCALE_GROUPS:
+                if before == c:
+                    for q in range(4):
+                        nc.sync.dma_start(
+                            out=w_pl[32 * q : 32 * q + 16, t0 * NT : t1 * NT].bitcast(I32),
+                            in_=s_i32[:, 4 * q : 4 * q + 4, t0 * NT // 4 : t1 * NT // 4],
+                        )
+            n0 = tiles[0] * NT
+            cols = len(tiles) * NT
+            if c == 0:
+                for g in range(G):
+                    wt = keep.tile([P, cols], U32, name="w0_%d" % g, align_bytes=64)
+                    nc.sync.dma_start(out=wt[:].bitcast(I32), in_=w_i32[g, :, n0 : n0 + cols])
+                    w_slice[(tiles[0], g)] = wt[:, 0:NT]
+            else:
+                wt = keep.tile([P, G, cols], U32, name="w%d" % c, align_bytes=64)
+                nc.sync.dma_start(
+                    out=wt[:].bitcast(I32),
+                    in_=w_i32[:, :, n0 : n0 + cols].rearrange("g p n -> p g n"),
+                )
+                for j, nt in enumerate(tiles):
+                    for g in range(G):
+                        w_slice[(nt, g)] = wt[:, g, j * NT : (j + 1) * NT]
+
+        def transposes(i):
+            xw = x_sb[i][:].bitcast(F32)
+            banks = []
+            for h in range(2):
+                tp = psum.tile([P, 2, 2, P], F32, tag="bank", name="tp")
+                for g2 in range(2):
+                    g = 2 * h + g2
+                    for u in range(2):
+                        nc.tensor.transpose(
+                            tp[:, g2, u, :], xw[:, 256 * g + u : 256 * (g + 1) : 2], ident[:]
+                        )
+                banks.append(tp)
+            return banks
+
+        def xcopy(i, h, tp, on_vector):
+            dst = grouped[i][:, 2 * h : 2 * h + 2, :, :].bitcast(F32)
+            src = tp[:].rearrange("p g u m -> p g m u")
+            if on_vector:
+                nc.vector.tensor_copy(out=dst, in_=src)
+            else:
+                nc.scalar.copy(out=dst, in_=src)
+
+        def quant(i, h):
+            nc.vector.quantize_mx(
+                out=x_codes[i][:, 256 * h : 256 * (h + 1)].bitcast(FP8X4),
+                scales=x_pl[i][:, 256 * h : 256 * (h + 1)],
+                in_=grouped[i][:, 2 * h : 2 * h + 2, :, :].rearrange("p g m t -> p (g m t)"),
+            )
+
+        def spread(piece):
+            a, b = BIAS_PIECES[piece]
+            nc.scalar.copy(
+                out=b_spread[:, a:b].rearrange("p (c i) -> p c i", i=32),
+                in_=bt_sb[:, a // 32 : b // 32].unsqueeze(2).to_broadcast([P, (b - a) // 32, 32]),
+            )
+
+        def flip(piece):
+            a, b = BIAS_PIECES[piece]
+            nc.vector.transpose(out=bias_bc[:, a:b], in_=b_spread[:, a:b])
+
+        def x_tile(i):
+            banks = transposes(i)
+            xcopy(i, 0, banks[0], True)
+            xcopy(i, 1, banks[1], False)
+
+        x_tile(0)
+        nc.vector.tensor_copy(
+            out=b_rep[:],
+            in_=b_raw[:].rearrange("c (h j) -> c h j", h=2).unsqueeze(2).to_broadcast([P, 2, 4, 32]),
+        )
+        x_tile(1)
+        bt_ps = psum.tile([P, 2, P], F32, tag="bank", name="bt_ps")
+        for h in range(2):
+            nc.tensor.transpose(
+                bt_ps[:, h, :], b_rep[:, h, :, :].rearrange("c a j -> c (a j)"), ident[:]
+            )
+        nc.scalar.copy(
+            out=bt_sb[:].rearrange("p (c h) -> p c h", h=2),
+            in_=bt_ps[:, :, 0:88].rearrange("p h c -> p c h"),
+        )
+        quant(0, 0)
+        quant(0, 1)
+        spread(0)
+        x_tile(2)
+        quant(1, 0)
+        quant(1, 1)
+        x_tile(3)
+        quant(2, 0)
+        quant(2, 1)
+        quant(3, 0)
+        quant(3, 1)
+        spread(1)
+        spread(2)
+        spread(3)
+        flip(0)
+        flip(1)
+
+        def mx_pass(acc, i, nt, g):
+            nc.tensor.matmul_mx(
+                out=acc[:],
+                lhsT=x_codes[i][:, g * P : (g + 1) * P].bitcast(FP8X4),
+                lhsT_scale=x_pl[i][:, g * P : (g + 1) * P],
+                rhs=w_slice[(nt, g)].bitcast(FP8X4),
+                rhs_scale=w_pl[4 * g : P, nt * NT : (nt + 1) * NT],
+                start=(g == 0),
+                stop=(g == G - 1),
+            )
+
+        slab_of = {}
+
+        def finish(acc, i, nt, store_now):
+            sg = [s for s in range(len(SLAB_GROUPS)) if nt in SLAB_GROUPS[s]][0]
+            first = SLAB_GROUPS[sg][0]
+            if (i, sg) not in slab_of:
+                slab_of[(i, sg)] = slabs.tile([P, 4 * NT], F32, tag="slab", name="slab")
+            slab = slab_of[(i, sg)]
+            off = (nt - first) * NT
+            nc.vector.tensor_tensor(
+                out=slab[:, off : off + NT],
+                in0=acc[:],
+                in1=bias_bc[:, nt * NT : (nt + 1) * NT],
+                op=ADD,
+            )
+            if store_now is not None:
+                t0, t1 = store_now
+                nc.sync.dma_start(
+                    out=out2d[i * P : (i + 1) * P, t0 * NT : t1 * NT],
+                    in_=slab[:, (t0 - first) * NT : (t1 - first) * NT],
+                )
+
+        accs = []
+        for i in range(MT):
+            accs.append(psum.tile([P, NT], F32, tag="bank", name="acc"))
+        for g in range(G):
+            for i in range(MT):
+                mx_pass(accs[i], i, 0, g)
+        for i in range(MT):
+            finish(accs[i], i, 0, None)
+        flip(2)
+
+        for nt in range(1, 8):
+            for i in range(MT):
+                acc = psum.tile([P, NT], F32, tag="bank", name="acc")
+                for g in range(G):
+                    mx_pass(acc, i, nt, g)
+                store = None
+                if nt == 3:
+                    store = (0, 4)
+                if nt == 7:
+                    store = (4, 8)
+                finish(acc, i, nt, store)
+            if nt == 1:
+                flip(3)
+
+        for i in range(MT):
+            for nt in range(8, NTILES):
+                acc = psum.tile([P, NT], F32, tag="bank", name="acc")
+                for g in range(G):
+                    mx_pass(acc, i, nt, g)
+                store = None
+                if i < MT - 1:
+                    if nt == NTILES - 1:
+                        store = (8, NTILES)
+                else:
+                    if nt == NTILES - 2:
+                        store = (8, NTILES - 1)
+                    if nt == NTILES - 1:
+                        store = (NTILES - 1, NTILES)
+                finish(acc, i, nt, store)

@@ -23,7 +23,7 @@ NTILES = N // NT
 FLOPS = 2 * M * K * N
 
 CHUNKS = [[0], [1], [2], [3, 4], [5, 6], [7, 8, 9, 10]]
-SCALE_GROUPS = [(0, 3, 0), (3, 7, 3), (7, 11, 4)]
+SCALE_QUADRANTS = [0, 2, 1, 3]
 SLAB_GROUPS = [[0, 1, 2, 3], [4, 5, 6, 7], [8, 9, 10]]
 BIAS_PIECES = [(0, 1024), (1024, 2048), (2048, 4096), (4096, 5632)]
 
@@ -33,7 +33,7 @@ def tile_mxlinear_kernel(tc, x_in, bias, w_words, w_scales, out):
     x2d = x_in.flatten_outer_dims()
     out2d = out.flatten_outer_dims()
     w_i32 = w_words.rearrange("g p n t -> g p (n t)").bitcast(I32)
-    s_i32 = w_scales.bitcast(I32)
+    s_f32 = w_scales.bitcast(F32)
 
     with ExitStack() as ctx:
         keep = ctx.enter_context(tc.tile_pool(name="keep", bufs=1))
@@ -58,9 +58,15 @@ def tile_mxlinear_kernel(tc, x_in, bias, w_words, w_scales, out):
             x_codes.append(keep.tile([P, G * P], U32, name="x_codes%d" % i, align_bytes=64))
             x_pl.append(keep.tile([P, G * P], U8, name="x_pl%d" % i, align_bytes=64))
 
-        nc.vector.memset(b_raw[:], 0.0)
+        nc.vector.memset(ident[:], 0.0)
         nc.vector.memset(w_pl[:].bitcast(I32), 0)
-        make_identity(nc, ident[:])
+        nc.vector.memset(b_raw[:], 0.0)
+        make_identity(nc, ident[:], nomemset=True)
+        for q in SCALE_QUADRANTS:
+            nc.gpsimd.dma_start(
+                out=w_pl[32 * q : 32 * q + 16, :].bitcast(F32),
+                in_=s_f32[:, 4 * q : 4 * q + 4, :],
+            )
         nc.scalar.dma_start(out=b_raw[0:88, :], in_=bias.rearrange("(c e) -> c e", e=64))
 
         for i in range(MT):
@@ -68,13 +74,6 @@ def tile_mxlinear_kernel(tc, x_in, bias, w_words, w_scales, out):
 
         w_slice = {}
         for c, tiles in enumerate(CHUNKS):
-            for t0, t1, before in SCALE_GROUPS:
-                if before == c:
-                    for q in range(4):
-                        nc.sync.dma_start(
-                            out=w_pl[32 * q : 32 * q + 16, t0 * NT : t1 * NT].bitcast(I32),
-                            in_=s_i32[:, 4 * q : 4 * q + 4, t0 * NT // 4 : t1 * NT // 4],
-                        )
             n0 = tiles[0] * NT
             cols = len(tiles) * NT
             if c == 0:

@@ -22,8 +22,11 @@ NTILES = N // NT
 
 FLOPS = 2 * M * K * N
 
+PAD = 48
+SLOT = 256
+
 CHUNKS = [[0], [1], [2], [3, 4], [5, 6], [7, 8, 9, 10]]
-SCALE_QUADRANTS = [0, 2, 1, 3]
+SCALE_GROUPS = [(0, 3, 0), (3, 7, 3), (7, 11, 4)]
 SLAB_GROUPS = [[0, 1, 2, 3], [4, 5, 6, 7], [8, 9, 10]]
 BIAS_PIECES = [(0, 1024), (1024, 2048), (2048, 4096), (4096, 5632)]
 
@@ -33,7 +36,7 @@ def tile_mxlinear_kernel(tc, x_in, bias, w_words, w_scales, out):
     x2d = x_in.flatten_outer_dims()
     out2d = out.flatten_outer_dims()
     w_i32 = w_words.rearrange("g p n t -> g p (n t)").bitcast(I32)
-    s_f32 = w_scales.bitcast(F32)
+    s_i32 = w_scales.bitcast(I32)
 
     with ExitStack() as ctx:
         keep = ctx.enter_context(tc.tile_pool(name="keep", bufs=1))
@@ -47,7 +50,7 @@ def tile_mxlinear_kernel(tc, x_in, bias, w_words, w_scales, out):
         bt_sb = keep.tile([P, N // 32], F32, name="bt_sb")
         b_spread = keep.tile([P, N], BF16, name="b_spread", align_bytes=64)
         bias_bc = keep.tile([P, N], BF16, name="bias_bc", align_bytes=64)
-        w_pl = keep.tile([P, N], U8, name="w_pl", align_bytes=64)
+        w_pl = keep.tile([P, N], U8, name="w_pl", align_bytes=256)
         x_sb = []
         grouped = []
         x_codes = []
@@ -55,18 +58,12 @@ def tile_mxlinear_kernel(tc, x_in, bias, w_words, w_scales, out):
         for i in range(MT):
             x_sb.append(keep.tile([P, K], BF16, name="x_sb%d" % i))
             grouped.append(keep.tile([P, G, P, 4], BF16, name="grouped%d" % i, align_bytes=64))
-            x_codes.append(keep.tile([P, G * P], U32, name="x_codes%d" % i, align_bytes=64))
-            x_pl.append(keep.tile([P, G * P], U8, name="x_pl%d" % i, align_bytes=64))
+            x_codes.append(keep.tile([P, PAD + G * P], U32, name="x_codes%d" % i, align_bytes=256))
+            x_pl.append(keep.tile([P, G * SLOT], U8, name="x_pl%d" % i, align_bytes=256))
 
-        nc.vector.memset(ident[:], 0.0)
-        nc.vector.memset(w_pl[:].bitcast(I32), 0)
         nc.vector.memset(b_raw[:], 0.0)
-        make_identity(nc, ident[:], nomemset=True)
-        for q in SCALE_QUADRANTS:
-            nc.gpsimd.dma_start(
-                out=w_pl[32 * q : 32 * q + 16, :].bitcast(F32),
-                in_=s_f32[:, 4 * q : 4 * q + 4, :],
-            )
+        nc.vector.memset(w_pl[:].bitcast(I32), 0)
+        make_identity(nc, ident[:])
         nc.scalar.dma_start(out=b_raw[0:88, :], in_=bias.rearrange("(c e) -> c e", e=64))
 
         for i in range(MT):
@@ -74,15 +71,22 @@ def tile_mxlinear_kernel(tc, x_in, bias, w_words, w_scales, out):
 
         w_slice = {}
         for c, tiles in enumerate(CHUNKS):
+            for t0, t1, before in SCALE_GROUPS:
+                if before == c:
+                    for q in range(4):
+                        nc.sync.dma_start(
+                            out=w_pl[32 * q : 32 * q + 16, t0 * NT : t1 * NT].bitcast(I32),
+                            in_=s_i32[:, 4 * q : 4 * q + 4, t0 * NT // 4 : t1 * NT // 4],
+                        )
             n0 = tiles[0] * NT
             cols = len(tiles) * NT
             if c == 0:
                 for g in range(G):
-                    wt = keep.tile([P, cols], U32, name="w0_%d" % g, align_bytes=64)
+                    wt = keep.tile([P, cols], U32, name="w0_%d" % g, align_bytes=256)
                     nc.sync.dma_start(out=wt[:].bitcast(I32), in_=w_i32[g, :, n0 : n0 + cols])
                     w_slice[(tiles[0], g)] = wt[:, 0:NT]
             else:
-                wt = keep.tile([P, G, cols], U32, name="w%d" % c, align_bytes=64)
+                wt = keep.tile([P, G, cols], U32, name="w%d" % c, align_bytes=256)
                 nc.sync.dma_start(
                     out=wt[:].bitcast(I32),
                     in_=w_i32[:, :, n0 : n0 + cols].rearrange("g p n -> p g n"),
@@ -114,11 +118,12 @@ def tile_mxlinear_kernel(tc, x_in, bias, w_words, w_scales, out):
                 nc.scalar.copy(out=dst, in_=src)
 
         def quant(i, h):
-            nc.vector.quantize_mx(
-                out=x_codes[i][:, 256 * h : 256 * (h + 1)].bitcast(FP8X4),
-                scales=x_pl[i][:, 256 * h : 256 * (h + 1)],
-                in_=grouped[i][:, 2 * h : 2 * h + 2, :, :].rearrange("p g m t -> p (g m t)"),
-            )
+            for g in (2 * h, 2 * h + 1):
+                nc.vector.quantize_mx(
+                    out=x_codes[i][:, PAD + g * P : PAD + (g + 1) * P].bitcast(FP8X4),
+                    scales=x_pl[i][:, g * SLOT : g * SLOT + P],
+                    in_=grouped[i][:, g, :, :].rearrange("p m t -> p (m t)"),
+                )
 
         def spread(piece):
             a, b = BIAS_PIECES[piece]
@@ -171,8 +176,8 @@ def tile_mxlinear_kernel(tc, x_in, bias, w_words, w_scales, out):
         def mx_pass(acc, i, nt, g):
             nc.tensor.matmul_mx(
                 out=acc[:],
-                lhsT=x_codes[i][:, g * P : (g + 1) * P].bitcast(FP8X4),
-                lhsT_scale=x_pl[i][:, g * P : (g + 1) * P],
+                lhsT=x_codes[i][:, PAD + g * P : PAD + (g + 1) * P].bitcast(FP8X4),
+                lhsT_scale=x_pl[i][:, g * SLOT : g * SLOT + P],
                 rhs=w_slice[(nt, g)].bitcast(FP8X4),
                 rhs_scale=w_pl[4 * g : P, nt * NT : (nt + 1) * NT],
                 start=(g == 0),

@@ -20,10 +20,9 @@ MT = M // P
 NT = 512
 NTILES = N // NT
 
-FLOPS = 2 * M * K * N
+JOBS = MT * NTILES
 
-PAD = 48
-SLOT = 256
+FLOPS = 2 * M * K * N
 
 CHUNKS = [[0], [1], [2], [3, 4], [5, 6], [7, 8, 9, 10]]
 SCALE_GROUPS = [(0, 3, 0), (3, 7, 3), (7, 11, 4)]
@@ -50,7 +49,7 @@ def tile_mxlinear_kernel(tc, x_in, bias, w_words, w_scales, out):
         bt_sb = keep.tile([P, N // 32], F32, name="bt_sb")
         b_spread = keep.tile([P, N], BF16, name="b_spread", align_bytes=64)
         bias_bc = keep.tile([P, N], BF16, name="bias_bc", align_bytes=64)
-        w_pl = keep.tile([P, N], U8, name="w_pl", align_bytes=256)
+        w_pl = keep.tile([P, N], U8, name="w_pl", align_bytes=64)
         x_sb = []
         grouped = []
         x_codes = []
@@ -58,8 +57,8 @@ def tile_mxlinear_kernel(tc, x_in, bias, w_words, w_scales, out):
         for i in range(MT):
             x_sb.append(keep.tile([P, K], BF16, name="x_sb%d" % i))
             grouped.append(keep.tile([P, G, P, 4], BF16, name="grouped%d" % i, align_bytes=64))
-            x_codes.append(keep.tile([P, PAD + G * P], U32, name="x_codes%d" % i, align_bytes=256))
-            x_pl.append(keep.tile([P, G * SLOT], U8, name="x_pl%d" % i, align_bytes=256))
+            x_codes.append(keep.tile([P, G * P], U32, name="x_codes%d" % i, align_bytes=64))
+            x_pl.append(keep.tile([P, G * P], U8, name="x_pl%d" % i, align_bytes=64))
 
         nc.vector.memset(b_raw[:], 0.0)
         nc.vector.memset(w_pl[:].bitcast(I32), 0)
@@ -82,11 +81,11 @@ def tile_mxlinear_kernel(tc, x_in, bias, w_words, w_scales, out):
             cols = len(tiles) * NT
             if c == 0:
                 for g in range(G):
-                    wt = keep.tile([P, cols], U32, name="w0_%d" % g, align_bytes=256)
+                    wt = keep.tile([P, cols], U32, name="w0_%d" % g, align_bytes=64)
                     nc.sync.dma_start(out=wt[:].bitcast(I32), in_=w_i32[g, :, n0 : n0 + cols])
                     w_slice[(tiles[0], g)] = wt[:, 0:NT]
             else:
-                wt = keep.tile([P, G, cols], U32, name="w%d" % c, align_bytes=256)
+                wt = keep.tile([P, G, cols], U32, name="w%d" % c, align_bytes=64)
                 nc.sync.dma_start(
                     out=wt[:].bitcast(I32),
                     in_=w_i32[:, :, n0 : n0 + cols].rearrange("g p n -> p g n"),
@@ -118,12 +117,11 @@ def tile_mxlinear_kernel(tc, x_in, bias, w_words, w_scales, out):
                 nc.scalar.copy(out=dst, in_=src)
 
         def quant(i, h):
-            for g in (2 * h, 2 * h + 1):
-                nc.vector.quantize_mx(
-                    out=x_codes[i][:, PAD + g * P : PAD + (g + 1) * P].bitcast(FP8X4),
-                    scales=x_pl[i][:, g * SLOT : g * SLOT + P],
-                    in_=grouped[i][:, g, :, :].rearrange("p m t -> p (m t)"),
-                )
+            nc.vector.quantize_mx(
+                out=x_codes[i][:, 256 * h : 256 * (h + 1)].bitcast(FP8X4),
+                scales=x_pl[i][:, 256 * h : 256 * (h + 1)],
+                in_=grouped[i][:, 2 * h : 2 * h + 2, :, :].rearrange("p g m t -> p (g m t)"),
+            )
 
         def spread(piece):
             a, b = BIAS_PIECES[piece]
@@ -168,16 +166,14 @@ def tile_mxlinear_kernel(tc, x_in, bias, w_words, w_scales, out):
         quant(3, 0)
         quant(3, 1)
         spread(1)
-        spread(2)
-        spread(3)
         flip(0)
         flip(1)
 
         def mx_pass(acc, i, nt, g):
             nc.tensor.matmul_mx(
                 out=acc[:],
-                lhsT=x_codes[i][:, PAD + g * P : PAD + (g + 1) * P].bitcast(FP8X4),
-                lhsT_scale=x_pl[i][:, g * SLOT : g * SLOT + P],
+                lhsT=x_codes[i][:, g * P : (g + 1) * P].bitcast(FP8X4),
+                lhsT_scale=x_pl[i][:, g * P : (g + 1) * P],
                 rhs=w_slice[(nt, g)].bitcast(FP8X4),
                 rhs_scale=w_pl[4 * g : P, nt * NT : (nt + 1) * NT],
                 start=(g == 0),
@@ -185,26 +181,35 @@ def tile_mxlinear_kernel(tc, x_in, bias, w_words, w_scales, out):
             )
 
         slab_of = {}
+        held = {"job": None}
 
-        def finish(acc, i, nt, store_now):
+        def store_cols(i, slab, first, cols):
+            if cols is not None:
+                t0, t1 = cols
+                nc.sync.dma_start(
+                    out=out2d[i * P : (i + 1) * P, t0 * NT : t1 * NT],
+                    in_=slab[:, (t0 - first) * NT : (t1 - first) * NT],
+                )
+
+        def finish(acc, i, nt, job, store_now):
             sg = [s for s in range(len(SLAB_GROUPS)) if nt in SLAB_GROUPS[s]][0]
             first = SLAB_GROUPS[sg][0]
             if (i, sg) not in slab_of:
                 slab_of[(i, sg)] = slabs.tile([P, 4 * NT], F32, tag="slab", name="slab")
             slab = slab_of[(i, sg)]
-            off = (nt - first) * NT
-            nc.vector.tensor_tensor(
-                out=slab[:, off : off + NT],
-                in0=acc[:],
-                in1=bias_bc[:, nt * NT : (nt + 1) * NT],
-                op=ADD,
-            )
-            if store_now is not None:
-                t0, t1 = store_now
-                nc.sync.dma_start(
-                    out=out2d[i * P : (i + 1) * P, t0 * NT : t1 * NT],
-                    in_=slab[:, (t0 - first) * NT : (t1 - first) * NT],
-                )
+            dst = slab[:, (nt - first) * NT : (nt - first + 1) * NT]
+            b = bias_bc[:, nt * NT : (nt + 1) * NT]
+            if job % 2 == 1 or job >= JOBS - 2:
+                nc.vector.tensor_tensor(out=dst, in0=acc[:], in1=b, op=ADD)
+                if held["job"] is not None:
+                    h_dst, h_b, h_i, h_slab, h_first, h_store = held["job"]
+                    nc.vector.tensor_tensor(out=h_dst, in0=h_dst, in1=h_b, op=ADD)
+                    store_cols(h_i, h_slab, h_first, h_store)
+                    held["job"] = None
+                store_cols(i, slab, first, store_now)
+            else:
+                nc.scalar.copy(out=dst, in_=acc[:])
+                held["job"] = (dst, b, i, slab, first, store_now)
 
         accs = []
         for i in range(MT):
@@ -213,8 +218,8 @@ def tile_mxlinear_kernel(tc, x_in, bias, w_words, w_scales, out):
             for i in range(MT):
                 mx_pass(accs[i], i, 0, g)
         for i in range(MT):
-            finish(accs[i], i, 0, None)
-        flip(2)
+            finish(accs[i], i, 0, i, None)
+        spread(2)
 
         for nt in range(1, 8):
             for i in range(MT):
@@ -226,8 +231,11 @@ def tile_mxlinear_kernel(tc, x_in, bias, w_words, w_scales, out):
                     store = (0, 4)
                 if nt == 7:
                     store = (4, 8)
-                finish(acc, i, nt, store)
+                finish(acc, i, nt, MT * nt + i, store)
             if nt == 1:
+                spread(3)
+                flip(2)
+            if nt == 2:
                 flip(3)
 
         for i in range(MT):
@@ -244,4 +252,4 @@ def tile_mxlinear_kernel(tc, x_in, bias, w_words, w_scales, out):
                         store = (8, NTILES - 1)
                     if nt == NTILES - 1:
                         store = (NTILES - 1, NTILES)
-                finish(acc, i, nt, store)
+                finish(acc, i, nt, MT * 8 + (NTILES - 8) * i + nt - 8, store)

from contextlib import ExitStack

import concourse.mybir as mybir
from concourse.masks import make_identity

F32 = mybir.dt.float32
BF16 = mybir.dt.bfloat16
I32 = mybir.dt.int32
U32 = mybir.dt.uint32
U8 = mybir.dt.uint8
FP8X4 = mybir.dt.float8_e4m3fn_x4
ADD = mybir.AluOpType.add

P = 128
M = 512
K = 2048
N = 5632
G = K // 512
MT = M // P
NT = 512
NTILES = N // NT

JOBS = MT * NTILES

FLOPS = 2 * M * K * N

CHUNKS = [[0], [1], [2], [3, 4], [5, 6], [7, 8, 9, 10]]
SCALE_GROUPS = [(0, 3, 0), (3, 7, 3), (7, 11, 4)]
SLAB_GROUPS = [[0, 1, 2, 3], [4, 5, 6, 7], [8, 9, 10]]
BIAS_PIECES = [(0, 1024), (1024, 2048), (2048, 4096), (4096, 5632)]


def tile_mxlinear_kernel(tc, x_in, bias, w_words, w_scales, out):
    nc = tc.nc
    x2d = x_in.flatten_outer_dims()
    out2d = out.flatten_outer_dims()
    w_i32 = w_words.rearrange("g p n t -> g p (n t)").bitcast(I32)
    s_i32 = w_scales.bitcast(I32)

    with ExitStack() as ctx:
        keep = ctx.enter_context(tc.tile_pool(name="keep", bufs=1))
        slabs = ctx.enter_context(tc.tile_pool(name="slabs", bufs=8))
        psum = ctx.enter_context(tc.psum_pool(name="psum", bufs=8))
        ctx.enter_context(tc.manual_schedule())

        ident = keep.tile([P, P], F32, name="ident")
        b_raw = keep.tile([P, 64], BF16, name="b_raw")
        b_rep = keep.tile([P, 2, 4, 32], F32, name="b_rep")
        bt_sb = keep.tile([P, N // 32], F32, name="bt_sb")
        b_spread = keep.tile([P, N], BF16, name="b_spread", align_bytes=64)
        bias_bc = keep.tile([P, N], BF16, name="bias_bc", align_bytes=64)
        w_pl = keep.tile([P, N], U8, name="w_pl", align_bytes=64)
        x_sb = []
        grouped = []
        x_codes = []
        x_pl = []
        for i in range(MT):
            x_sb.append(keep.tile([P, K], BF16, name="x_sb%d" % i))
            grouped.append(keep.tile([P, G, P, 4], BF16, name="grouped%d" % i, align_bytes=64))
            x_codes.append(keep.tile([P, G * P], U32, name="x_codes%d" % i, align_bytes=64))
            x_pl.append(keep.tile([P, G * P], U8, name="x_pl%d" % i, align_bytes=64))

        nc.vector.memset(b_raw[:], 0.0)
        nc.vector.memset(w_pl[:].bitcast(I32), 0)
        make_identity(nc, ident[:])
        nc.scalar.dma_start(out=b_raw[0:88, :], in_=bias.rearrange("(c e) -> c e", e=64))

        for i in range(MT):
            nc.sync.dma_start(out=x_sb[i][:], in_=x2d[i * P : (i + 1) * P, :])

        w_slice = {}
        for c, tiles in enumerate(CHUNKS):
            for t0, t1, before in SCALE_GROUPS:
                if before == c:
                    for q in range(4):
                        nc.sync.dma_start(
                            out=w_pl[32 * q : 32 * q + 16, t0 * NT : t1 * NT].bitcast(I32),
                            in_=s_i32[:, 4 * q : 4 * q + 4, t0 * NT // 4 : t1 * NT // 4],
                        )
            n0 = tiles[0] * NT
            cols = len(tiles) * NT
            if c == 0:
                for g in range(G):
                    wt = keep.tile([P, cols], U32, name="w0_%d" % g, align_bytes=64)
                    nc.sync.dma_start(out=wt[:].bitcast(I32), in_=w_i32[g, :, n0 : n0 + cols])
                    w_slice[(tiles[0], g)] = wt[:, 0:NT]
            else:
                wt = keep.tile([P, G, cols], U32, name="w%d" % c, align_bytes=64)
                nc.sync.dma_start(
                    out=wt[:].bitcast(I32),
                    in_=w_i32[:, :, n0 : n0 + cols].rearrange("g p n -> p g n"),
                )
                for j, nt in enumerate(tiles):
                    for g in range(G):
                        w_slice[(nt, g)] = wt[:, g, j * NT : (j + 1) * NT]

        def transposes(i):
            xw = x_sb[i][:].bitcast(F32)
            banks = []
            for h in range(2):
                tp = psum.tile([P, 2, 2, P], F32, tag="bank", name="tp")
                for g2 in range(2):
                    g = 2 * h + g2
                    for u in range(2):
                        nc.tensor.transpose(
                            tp[:, g2, u, :], xw[:, 256 * g + u : 256 * (g + 1) : 2], ident[:]
                        )
                banks.append(tp)
            return banks

        def xcopy(i, h, tp, on_vector):
            dst = grouped[i][:, 2 * h : 2 * h + 2, :, :].bitcast(F32)
            src = tp[:].rearrange("p g u m -> p g m u")
            if on_vector:
                nc.vector.tensor_copy(out=dst, in_=src)
            else:
                nc.scalar.copy(out=dst, in_=src)

        def quant(i, h):
            nc.vector.quantize_mx(
                out=x_codes[i][:, 256 * h : 256 * (h + 1)].bitcast(FP8X4),
                scales=x_pl[i][:, 256 * h : 256 * (h + 1)],
                in_=grouped[i][:, 2 * h : 2 * h + 2, :, :].rearrange("p g m t -> p (g m t)"),
            )

        def spread(piece):
            a, b = BIAS_PIECES[piece]
            nc.scalar.copy(
                out=b_spread[:, a:b].rearrange("p (c i) -> p c i", i=32),
                in_=bt_sb[:, a // 32 : b // 32].unsqueeze(2).to_broadcast([P, (b - a) // 32, 32]),
            )

        def flip(piece):
            a, b = BIAS_PIECES[piece]
            nc.vector.transpose(out=bias_bc[:, a:b], in_=b_spread[:, a:b])

        def x_tile(i):
            banks = transposes(i)
            xcopy(i, 0, banks[0], True)
            xcopy(i, 1, banks[1], False)

        x_tile(0)
        nc.vector.tensor_copy(
            out=b_rep[:],
            in_=b_raw[:].rearrange("c (h j) -> c h j", h=2).unsqueeze(2).to_broadcast([P, 2, 4, 32]),
        )
        x_tile(1)
        bt_ps = psum.tile([P, 2, P], F32, tag="bank", name="bt_ps")
        for h in range(2):
            nc.tensor.transpose(
                bt_ps[:, h, :], b_rep[:, h, :, :].rearrange("c a j -> c (a j)"), ident[:]
            )
        nc.scalar.copy(
            out=bt_sb[:].rearrange("p (c h) -> p c h", h=2),
            in_=bt_ps[:, :, 0:88].rearrange("p h c -> p c h"),
        )
        quant(0, 0)
        quant(0, 1)
        spread(0)
        x_tile(2)
        quant(1, 0)
        quant(1, 1)
        x_tile(3)
        quant(2, 0)
        quant(2, 1)
        quant(3, 0)
        quant(3, 1)
        spread(1)
        flip(0)
        flip(1)

        def mx_pass(acc, i, nt, g):
            nc.tensor.matmul_mx(
                out=acc[:],
                lhsT=x_codes[i][:, g * P : (g + 1) * P].bitcast(FP8X4),
                lhsT_scale=x_pl[i][:, g * P : (g + 1) * P],
                rhs=w_slice[(nt, g)].bitcast(FP8X4),
                rhs_scale=w_pl[4 * g : P, nt * NT : (nt + 1) * NT],
                start=(g == 0),
                stop=(g == G - 1),
            )

        slab_of = {}
        held = {"job": None}

        def store_cols(i, slab, first, cols):
            if cols is not None:
                t0, t1 = cols
                nc.sync.dma_start(
                    out=out2d[i * P : (i + 1) * P, t0 * NT : t1 * NT],
                    in_=slab[:, (t0 - first) * NT : (t1 - first) * NT],
                )

        def finish(acc, i, nt, job, store_now):
            sg = [s for s in range(len(SLAB_GROUPS)) if nt in SLAB_GROUPS[s]][0]
            first = SLAB_GROUPS[sg][0]
            if (i, sg) not in slab_of:
                slab_of[(i, sg)] = slabs.tile([P, 4 * NT], F32, tag="slab", name="slab")
            slab = slab_of[(i, sg)]
            dst = slab[:, (nt - first) * NT : (nt - first + 1) * NT]
            b = bias_bc[:, nt * NT : (nt + 1) * NT]
            if job % 2 == 1 or job >= JOBS - 2:
                nc.vector.tensor_tensor(out=dst, in0=acc[:], in1=b, op=ADD)
                if held["job"] is not None:
                    h_dst, h_b, h_i, h_slab, h_first, h_store = held["job"]
                    nc.vector.tensor_tensor(out=h_dst, in0=h_dst, in1=h_b, op=ADD)
                    store_cols(h_i, h_slab, h_first, h_store)
                    held["job"] = None
                store_cols(i, slab, first, store_now)
            else:
                nc.scalar.copy(out=dst, in_=acc[:])
                held["job"] = (dst, b, i, slab, first, store_now)

        accs = []
        for i in range(MT):
            accs.append(psum.tile([P, NT], F32, tag="bank", name="acc"))
        for g in range(G):
            for i in range(MT):
                mx_pass(accs[i], i, 0, g)
        for i in range(MT):
            finish(accs[i], i, 0, i, None)
        spread(2)

        for nt in range(1, 8):
            for i in range(MT):
                acc = psum.tile([P, NT], F32, tag="bank", name="acc")
                for g in range(G):
                    mx_pass(acc, i, nt, g)
                store = None
                if nt == 3:
                    store = (0, 4)
                if nt == 7:
                    store = (4, 8)
                finish(acc, i, nt, MT * nt + i, store)
            if nt == 1:
                spread(3)
                flip(2)
            if nt == 2:
                flip(3)

        for i in range(MT):
            for nt in range(8, NTILES):
                acc = psum.tile([P, NT], F32, tag="bank", name="acc")
                for g in range(G):
                    mx_pass(acc, i, nt, g)
                store = None
                if i < MT - 1:
                    if nt == NTILES - 1:
                        store = (8, NTILES)
                else:
                    if nt == NTILES - 2:
                        store = (8, NTILES - 1)
                    if nt == NTILES - 1:
                        store = (NTILES - 1, NTILES)
                finish(acc, i, nt, MT * 8 + (NTILES - 8) * i + nt - 8, store)
